import numpy as np
import ml_dtypes


def mxq(x, axis, fmt="e4m3"):
    dtype, down = {"e4m3": (ml_dtypes.float8_e4m3fn, 7), "e5m2": (ml_dtypes.float8_e5m2, 14)}[fmt]
    v = np.moveaxis(np.asarray(x, np.float32).astype(ml_dtypes.bfloat16).astype(np.float64), axis, -1)
    blocks = v.reshape(v.shape[:-1] + (-1, 32))
    amax = np.abs(blocks).max(-1, keepdims=True)
    byte = np.maximum(np.where(amax > 0, np.frexp(amax)[1] - 1 + 127, 0) - down, 1)
    scale = np.exp2(byte - 127.0)
    codes = (blocks / scale).astype(np.float32).astype(dtype).astype(np.float64)
    return np.moveaxis((codes * scale).reshape(v.shape), -1, axis)


WIDE = False


def mx_kscale(k):
    if not WIDE:
        return np.ones(k)
    levels = np.array([20, -20, 10, -10, 0])
    a = np.random.permutation(np.resize(levels, k // 512 * 4)).reshape(k // 512, 4)
    idx = np.arange(k)
    return np.exp2(a[idx // 512, idx % 128 // 32])


BF16 = ml_dtypes.bfloat16


def bf(x):
    return np.asarray(x, np.float32).astype(BF16)


def f64(x):
    return np.asarray(x).astype(np.float64)


B, A, C, P = 512, 1, 512, 512
N = A * A + 1
T = B * N


def scramble(y):
    return y.transpose(0, 2, 1).reshape(B, N, C)


def unscramble(z):
    return z.reshape(B, C, N).transpose(0, 2, 1)


def setup_inputs():
    s = mx_kscale(T).reshape(B, N, 1)
    z = np.random.standard_normal((B, N, C)) * 1.6 / np.sqrt(N) * s
    w = np.random.standard_normal((P, C)) * 2.0 / np.sqrt(C)
    b = np.random.standard_normal(P) * 0.1
    g = np.random.standard_normal((B, N, P)) * np.exp2(np.random.randint(-12, 1, (B, N, 1))) / s
    return {"y_attn": bf(np.ascontiguousarray(unscramble(z))),
            "w_proj": bf(w),
            "b_proj": bf(b),
            "grad_out": bf(g)}


def reference(y_attn, w_proj, b_proj, grad_out):
    z = scramble(f64(y_attn)).reshape(T, C)
    g = f64(grad_out).reshape(T, P)
    return mxq(g, 0, "e5m2").T @ mxq(z, 0, "e4m3")

@@ -1,0 +1,112 @@
+from contextlib import ExitStack
+
+import concourse.mybir as mybir
+
+BF16 = mybir.dt.bfloat16
+F32 = mybir.dt.float32
+U32 = mybir.dt.uint32
+U8 = mybir.dt.uint8
+E4M3_X4 = mybir.dt.float8_e4m3fn_x4
+E5M2_X4 = mybir.dt.float8_e5m2_x4
+
+P = 128
+PACK = 4
+K_PASS = P * PACK
+IMAGES = 512
+TOKENS = 2
+WIDTH = 512
+ROWS = IMAGES * TOKENS
+PASSES = ROWS // K_PASS
+IMAGES_PER_PARTITION = PACK // TOKENS
+HALF = WIDTH // 2
+F_TILES = WIDTH // P
+
+FLOPS = 2 * ROWS * WIDTH * WIDTH
+BYTES = 2 * ROWS * WIDTH * 2 + WIDTH * WIDTH * 4
+
+
+def regroup(copy, grouped, rows):
+    copy(
+        out=grouped.rearrange("p (c r) s -> p c s r", r=4),
+        in_=rows.rearrange("p s (c r) -> p c s r", r=4),
+    )
+
+
+def tile_attention_pa_s_kernel(tc, y_attn, w_proj, b_proj, grad_out, out):
+    nc = tc.nc
+    g_rows = grad_out.rearrange("b i f -> (b i) f")
+
+    with ExitStack() as ctx:
+        keep = ctx.enter_context(tc.tile_pool(name="keep", bufs=1))
+        psum = ctx.enter_context(tc.psum_pool(name="psum", bufs=1))
+
+        z_raw = keep.tile([P, PASSES, TOKENS, PACK, HALF], BF16)
+        g_raw = keep.tile([P, PASSES, PACK, WIDTH], BF16)
+        z_grouped = keep.tile([P, PASSES, WIDTH, PACK], BF16, align_bytes=64)
+        g_grouped = keep.tile([P, PASSES, WIDTH, PACK], BF16, align_bytes=64)
+        z_codes = keep.tile([P, PASSES, WIDTH], U32, align_bytes=64)
+        z_scales = keep.tile([P, PASSES, WIDTH], U8, align_bytes=64)
+        g_codes = keep.tile([P, PASSES, WIDTH], U32, align_bytes=64)
+        g_scales = keep.tile([P, PASSES, WIDTH], U8, align_bytes=64)
+
+        for c in range(PASSES):
+            images = slice(c * K_PASS // TOKENS, (c + 1) * K_PASS // TOKENS)
+            for parity in range(TOKENS):
+                nc.sync.dma_start(
+                    out=z_raw[:, c, parity].rearrange(
+                        "p (m i) h -> p m i h", m=IMAGES_PER_PARTITION
+                    ),
+                    in_=y_attn[images, parity, :].rearrange(
+                        "(p m) (i h) -> p m i h", m=IMAGES_PER_PARTITION, i=TOKENS
+                    ),
+                )
+            nc.sync.dma_start(
+                out=g_raw[:, c],
+                in_=g_rows[c * K_PASS : (c + 1) * K_PASS, :].rearrange(
+                    "(p s) f -> p s f", s=PACK
+                ),
+            )
+
+        acc = [psum.tile([P, WIDTH], F32, name="acc%d" % f) for f in range(F_TILES)]
+
+        copies = [nc.vector.tensor_copy, nc.scalar.copy]
+        for c in range(PASSES):
+            for half in range(2):
+                cols = slice(half * HALF, (half + 1) * HALF)
+                regroup(copies[half], z_grouped[:, c, cols, :], z_raw[:, c, half])
+            for half in range(2):
+                cols = slice(half * HALF, (half + 1) * HALF)
+                regroup(copies[half], g_grouped[:, c, cols, :], g_raw[:, c, :, cols])
+            for half in range(2):
+                cols = slice(half * HALF, (half + 1) * HALF)
+                nc.vector.quantize_mx(
+                    out=z_codes[:, c, cols].bitcast(E4M3_X4),
+                    scales=z_scales[:, c, cols],
+                    in_=z_grouped[:, c, cols, :].rearrange("p w s -> p (w s)"),
+                )
+            for half in range(2):
+                cols = slice(half * HALF, (half + 1) * HALF)
+                nc.vector.quantize_mx(
+                    out=g_codes[:, c, cols].bitcast(E5M2_X4),
+                    scales=g_scales[:, c, cols],
+                    in_=g_grouped[:, c, cols, :].rearrange("p w s -> p (w s)"),
+                )
+            for f in range(F_TILES):
+                f_cols = slice(f * P, (f + 1) * P)
+                nc.tensor.matmul_mx(
+                    out=acc[f][:],
+                    lhsT=g_codes[:, c, f_cols].bitcast(E5M2_X4),
+                    lhsT_scale=g_scales[:, c, f_cols],
+                    rhs=z_codes[:, c, :].bitcast(E4M3_X4),
+                    rhs_scale=z_scales[:, c, :],
+                    start=(c == 0),
+                    stop=(c == PASSES - 1),
+                )
+
+        for f in range(F_TILES):
+            result = keep.tile([P, WIDTH], F32, name="result%d" % f)
+            copies[(f + 1) % 2](
+                out=result[:].rearrange("p (h n) -> p h n", n=TOKENS),
+                in_=acc[f][:].rearrange("p (n h) -> p h n", n=TOKENS),
+            )
+            nc.sync.dma_start(out=out[f * P : (f + 1) * P, :], in_=result[:])

@@ -39,6 +39,7 @@ def tile_attention_pa_s_kernel(tc, y_attn, w_proj, b_proj, grad_out, out):
     with ExitStack() as ctx:
         keep = ctx.enter_context(tc.tile_pool(name="keep", bufs=1))
         psum = ctx.enter_context(tc.psum_pool(name="psum", bufs=1))
+        ctx.enter_context(tc.manual_schedule())
 
         z_raw = keep.tile([P, PASSES, TOKENS, PACK, HALF], BF16)
         g_raw = keep.tile([P, PASSES, PACK, WIDTH], BF16)
@@ -48,6 +49,7 @@ def tile_attention_pa_s_kernel(tc, y_attn, w_proj, b_proj, grad_out, out):
         z_scales = keep.tile([P, PASSES, WIDTH], U8, align_bytes=64)
         g_codes = keep.tile([P, PASSES, WIDTH], U32, align_bytes=64)
         g_scales = keep.tile([P, PASSES, WIDTH], U8, align_bytes=64)
+        acc = [psum.tile([P, WIDTH], F32, name="acc%d" % f) for f in range(F_TILES)]
 
         for c in range(PASSES):
             images = slice(c * K_PASS // TOKENS, (c + 1) * K_PASS // TOKENS)
@@ -67,46 +69,59 @@ def tile_attention_pa_s_kernel(tc, y_attn, w_proj, b_proj, grad_out, out):
                 ),
             )
 
-        acc = [psum.tile([P, WIDTH], F32, name="acc%d" % f) for f in range(F_TILES)]
+        def regroup_piece(copy, operand, c, index):
+            if operand == "z":
+                cols = slice(index * HALF, (index + 1) * HALF)
+                regroup(copy, z_grouped[:, c, cols, :], z_raw[:, c, index])
+            else:
+                cols = slice(index * P, (index + 1) * P)
+                regroup(copy, g_grouped[:, c, cols, :], g_raw[:, c, :, cols])
 
-        copies = [nc.vector.tensor_copy, nc.scalar.copy]
-        for c in range(PASSES):
-            for half in range(2):
-                cols = slice(half * HALF, (half + 1) * HALF)
-                regroup(copies[half], z_grouped[:, c, cols, :], z_raw[:, c, half])
-            for half in range(2):
-                cols = slice(half * HALF, (half + 1) * HALF)
-                regroup(copies[half], g_grouped[:, c, cols, :], g_raw[:, c, :, cols])
-            for half in range(2):
-                cols = slice(half * HALF, (half + 1) * HALF)
+        def quantise_piece(operand, c, index):
+            if operand == "z":
+                cols = slice(index * HALF, (index + 1) * HALF)
                 nc.vector.quantize_mx(
                     out=z_codes[:, c, cols].bitcast(E4M3_X4),
                     scales=z_scales[:, c, cols],
                     in_=z_grouped[:, c, cols, :].rearrange("p w s -> p (w s)"),
                 )
-            for half in range(2):
-                cols = slice(half * HALF, (half + 1) * HALF)
+            else:
+                cols = slice(index * P, (index + 1) * P)
                 nc.vector.quantize_mx(
                     out=g_codes[:, c, cols].bitcast(E5M2_X4),
                     scales=g_scales[:, c, cols],
                     in_=g_grouped[:, c, cols, :].rearrange("p w s -> p (w s)"),
                 )
-            for f in range(F_TILES):
-                f_cols = slice(f * P, (f + 1) * P)
                 nc.tensor.matmul_mx(
-                    out=acc[f][:],
-                    lhsT=g_codes[:, c, f_cols].bitcast(E5M2_X4),
-                    lhsT_scale=g_scales[:, c, f_cols],
+                    out=acc[index][:],
+                    lhsT=g_codes[:, c, cols].bitcast(E5M2_X4),
+                    lhsT_scale=g_scales[:, c, cols],
                     rhs=z_codes[:, c, :].bitcast(E4M3_X4),
                     rhs_scale=z_scales[:, c, :],
                     start=(c == 0),
                     stop=(c == PASSES - 1),
                 )
 
+        pieces = []
+        for c in range(PASSES):
+            pieces.extend(("z", c, parity) for parity in range(TOKENS))
+            pieces.extend(("g", c, f) for f in range(F_TILES))
+
+        copies = [nc.vector.tensor_copy, nc.scalar.copy]
+        for k, piece in enumerate(pieces):
+            regroup_piece(copies[k % 2], *piece)
+            if k > 0:
+                quantise_piece(*pieces[k - 1])
+        quantise_piece(*pieces[-1])
+
         for f in range(F_TILES):
             result = keep.tile([P, WIDTH], F32, name="result%d" % f)
-            copies[(f + 1) % 2](
-                out=result[:].rearrange("p (h n) -> p h n", n=TOKENS),
-                in_=acc[f][:].rearrange("p (n h) -> p h n", n=TOKENS),
-            )
-            nc.sync.dma_start(out=out[f * P : (f + 1) * P, :], in_=result[:])
+            by_parity = acc[f][:].rearrange("p (n h) -> p h n", n=TOKENS)
+            for part in range(2):
+                j_cols = slice(part * HALF, (part + 1) * HALF)
+                h_cols = slice(part * HALF // TOKENS, (part + 1) * HALF // TOKENS)
+                copies[(f + 1) % 2](
+                    out=result[:, j_cols].rearrange("p (h n) -> p h n", n=TOKENS),
+                    in_=by_parity[:, h_cols, :],
+                )
+                nc.sync.dma_start(out=out[f * P : (f + 1) * P, j_cols], in_=result[:, j_cols])

@@ -27,22 +27,21 @@ BYTES = 2 * ROWS * WIDTH * 2 + WIDTH * WIDTH * 4
 
 def regroup(copy, grouped, rows):
     copy(
-        out=grouped.rearrange("p (c r) s -> p c s r", r=4),
-        in_=rows.rearrange("p s (c r) -> p c s r", r=4),
+        out=grouped.rearrange("p (c r) (m i) -> p c m i r", r=4, i=TOKENS),
+        in_=rows.rearrange("p m i (c r) -> p c m i r", r=4),
     )
 
 
 def tile_attention_pa_s_kernel(tc, y_attn, w_proj, b_proj, grad_out, out):
     nc = tc.nc
-    g_rows = grad_out.rearrange("b i f -> (b i) f")
 
     with ExitStack() as ctx:
         keep = ctx.enter_context(tc.tile_pool(name="keep", bufs=1))
         psum = ctx.enter_context(tc.psum_pool(name="psum", bufs=1))
         ctx.enter_context(tc.manual_schedule())
 
-        z_raw = keep.tile([P, PASSES, TOKENS, PACK, HALF], BF16)
-        g_raw = keep.tile([P, PASSES, PACK, WIDTH], BF16)
+        z_raw = keep.tile([P, PASSES, IMAGES_PER_PARTITION, TOKENS, TOKENS, HALF], BF16)
+        g_raw = keep.tile([P, PASSES, IMAGES_PER_PARTITION, TOKENS, WIDTH], BF16)
         z_grouped = keep.tile([P, PASSES, WIDTH, PACK], BF16, align_bytes=64)
         g_grouped = keep.tile([P, PASSES, WIDTH, PACK], BF16, align_bytes=64)
         z_codes = keep.tile([P, PASSES, WIDTH], U32, align_bytes=64)
@@ -53,29 +52,22 @@ def tile_attention_pa_s_kernel(tc, y_attn, w_proj, b_proj, grad_out, out):
 
         for c in range(PASSES):
             images = slice(c * K_PASS // TOKENS, (c + 1) * K_PASS // TOKENS)
-            for parity in range(TOKENS):
-                nc.sync.dma_start(
-                    out=z_raw[:, c, parity].rearrange(
-                        "p (m i) h -> p m i h", m=IMAGES_PER_PARTITION
-                    ),
-                    in_=y_attn[images, parity, :].rearrange(
-                        "(p m) (i h) -> p m i h", m=IMAGES_PER_PARTITION, i=TOKENS
-                    ),
-                )
             nc.sync.dma_start(
-                out=g_raw[:, c],
-                in_=g_rows[c * K_PASS : (c + 1) * K_PASS, :].rearrange(
-                    "(p s) f -> p s f", s=PACK
-                ),
+                out=z_raw[:, c].rearrange("p m n i h -> p (m n i h)"),
+                in_=y_attn[images].rearrange("(p m) n x -> p (m n x)", m=IMAGES_PER_PARTITION),
+            )
+            nc.sync.dma_start(
+                out=g_raw[:, c].rearrange("p m i f -> p (m i f)"),
+                in_=grad_out[images].rearrange("(p m) i f -> p (m i f)", m=IMAGES_PER_PARTITION),
             )
 
         def regroup_piece(copy, operand, c, index):
             if operand == "z":
                 cols = slice(index * HALF, (index + 1) * HALF)
-                regroup(copy, z_grouped[:, c, cols, :], z_raw[:, c, index])
+                regroup(copy, z_grouped[:, c, cols, :], z_raw[:, c, :, index])
             else:
                 cols = slice(index * P, (index + 1) * P)
-                regroup(copy, g_grouped[:, c, cols, :], g_raw[:, c, :, cols])
+                regroup(copy, g_grouped[:, c, cols, :], g_raw[:, c, :, :, cols])
 
         def quantise_piece(operand, c, index):
             if operand == "z":

@@ -56,6 +56,8 @@ def tile_attention_pa_s_kernel(tc, y_attn, w_proj, b_proj, grad_out, out):
                 out=z_raw[:, c].rearrange("p m n i h -> p (m n i h)"),
                 in_=y_attn[images].rearrange("(p m) n x -> p (m n x)", m=IMAGES_PER_PARTITION),
             )
+        for c in range(PASSES):
+            images = slice(c * K_PASS // TOKENS, (c + 1) * K_PASS // TOKENS)
             nc.sync.dma_start(
                 out=g_raw[:, c].rearrange("p m i f -> p (m i f)"),
                 in_=grad_out[images].rearrange("(p m) i f -> p (m i f)", m=IMAGES_PER_PARTITION),
@@ -94,26 +96,51 @@ def tile_attention_pa_s_kernel(tc, y_attn, w_proj, b_proj, grad_out, out):
                     stop=(c == PASSES - 1),
                 )
 
-        pieces = []
-        for c in range(PASSES):
-            pieces.extend(("z", c, parity) for parity in range(TOKENS))
-            pieces.extend(("g", c, f) for f in range(F_TILES))
-
-        copies = [nc.vector.tensor_copy, nc.scalar.copy]
-        for k, piece in enumerate(pieces):
-            regroup_piece(copies[k % 2], *piece)
-            if k > 0:
-                quantise_piece(*pieces[k - 1])
-        quantise_piece(*pieces[-1])
-
-        for f in range(F_TILES):
+        def leave(copy, f):
             result = keep.tile([P, WIDTH], F32, name="result%d" % f)
             by_parity = acc[f][:].rearrange("p (n h) -> p h n", n=TOKENS)
             for part in range(2):
                 j_cols = slice(part * HALF, (part + 1) * HALF)
                 h_cols = slice(part * HALF // TOKENS, (part + 1) * HALF // TOKENS)
-                copies[(f + 1) % 2](
+                copy(
                     out=result[:, j_cols].rearrange("p (h n) -> p h n", n=TOKENS),
                     in_=by_parity[:, h_cols, :],
                 )
                 nc.sync.dma_start(out=out[f * P : (f + 1) * P, j_cols], in_=result[:, j_cols])
+
+        vector = nc.vector.tensor_copy
+        scalar = nc.scalar.copy
+
+        idle = psum.tile([P, WIDTH], F32, name="idle")
+        some_rows = z_raw[:, 1, 0, 0].rearrange("p i h -> p (i h)")
+        for repeat in range(3):
+            nc.tensor.matmul(out=idle[:], lhsT=some_rows[:, 0:P], rhs=some_rows, start=True, stop=True)
+
+        regroup_piece(vector, "z", 0, 0)
+        regroup_piece(scalar, "z", 0, 1)
+        quantise_piece("z", 0, 0)
+        regroup_piece(vector, "z", 1, 0)
+        quantise_piece("z", 0, 1)
+        regroup_piece(scalar, "z", 1, 1)
+        quantise_piece("z", 1, 0)
+        regroup_piece(vector, "g", 0, 0)
+        quantise_piece("z", 1, 1)
+        regroup_piece(scalar, "g", 0, 1)
+        regroup_piece(vector, "g", 1, 0)
+        quantise_piece("g", 0, 0)
+        quantise_piece("g", 1, 0)
+        regroup_piece(scalar, "g", 1, 1)
+        quantise_piece("g", 0, 1)
+        regroup_piece(vector, "g", 0, 2)
+        quantise_piece("g", 1, 1)
+        regroup_piece(scalar, "g", 0, 3)
+        regroup_piece(vector, "g", 1, 2)
+        quantise_piece("g", 0, 2)
+        quantise_piece("g", 1, 2)
+        leave(scalar, 0)
+        regroup_piece(vector, "g", 1, 3)
+        quantise_piece("g", 0, 3)
+        leave(scalar, 1)
+        quantise_piece("g", 1, 3)
+        leave(scalar, 2)
+        leave(vector, 3)

@@ -20,6 +20,7 @@ PASSES = ROWS // K_PASS
 IMAGES_PER_PARTITION = PACK // TOKENS
 HALF = WIDTH // 2
 F_TILES = WIDTH // P
+IDLE_PASSES = 13
 
 FLOPS = 2 * ROWS * WIDTH * WIDTH
 BYTES = 2 * ROWS * WIDTH * 2 + WIDTH * WIDTH * 4
@@ -111,10 +112,29 @@ def tile_attention_pa_s_kernel(tc, y_attn, w_proj, b_proj, grad_out, out):
         vector = nc.vector.tensor_copy
         scalar = nc.scalar.copy
 
+        zeros = keep.tile([P, P * PACK], BF16, align_bytes=64)
+        idle_z_codes = keep.tile([P, WIDTH], U32, align_bytes=64)
+        idle_z_scales = keep.tile([P, WIDTH], U8, align_bytes=64)
+        idle_g_codes = keep.tile([P, P], U32, align_bytes=64)
+        idle_g_scales = keep.tile([P, P], U8, align_bytes=64)
         idle = psum.tile([P, WIDTH], F32, name="idle")
-        some_rows = z_raw[:, 1, 0, 0].rearrange("p i h -> p (i h)")
-        for repeat in range(3):
-            nc.tensor.matmul(out=idle[:], lhsT=some_rows[:, 0:P], rhs=some_rows, start=True, stop=True)
+        nc.vector.memset(zeros[:], 0.0)
+        nc.vector.quantize_mx(out=idle_g_codes[:].bitcast(E5M2_X4), scales=idle_g_scales[:], in_=zeros[:])
+        for f in range(F_TILES):
+            cols = slice(f * P, (f + 1) * P)
+            nc.vector.quantize_mx(
+                out=idle_z_codes[:, cols].bitcast(E4M3_X4), scales=idle_z_scales[:, cols], in_=zeros[:]
+            )
+        for repeat in range(IDLE_PASSES):
+            nc.tensor.matmul_mx(
+                out=idle[:],
+                lhsT=idle_g_codes[:].bitcast(E5M2_X4),
+                lhsT_scale=idle_g_scales[:],
+                rhs=idle_z_codes[:].bitcast(E4M3_X4),
+                rhs_scale=idle_z_scales[:],
+                start=True,
+                stop=True,
+            )
 
         regroup_piece(vector, "z", 0, 0)
         regroup_piece(scalar, "z", 0, 1)

@@ -41,8 +41,10 @@ def tile_attention_pa_s_kernel(tc, y_attn, w_proj, b_proj, grad_out, out):
         psum = ctx.enter_context(tc.psum_pool(name="psum", bufs=1))
         ctx.enter_context(tc.manual_schedule())
 
-        z_raw = keep.tile([P, PASSES, IMAGES_PER_PARTITION, TOKENS, TOKENS, HALF], BF16)
-        g_raw = keep.tile([P, PASSES, IMAGES_PER_PARTITION, TOKENS, WIDTH], BF16)
+        z_raw0 = keep.tile([P, IMAGES_PER_PARTITION, TOKENS, TOKENS, HALF], BF16, name="z_raw0")
+        g_raw0 = keep.tile([P, IMAGES_PER_PARTITION, TOKENS, WIDTH], BF16, name="g_raw0")
+        z_raw1 = keep.tile([P, IMAGES_PER_PARTITION, TOKENS, TOKENS, HALF], BF16, name="z_raw1")
+        g_raw1 = [keep.tile([P, IMAGES_PER_PARTITION, TOKENS, HALF], BF16, name="g_raw1_%d" % side) for side in range(2)]
         z_grouped = keep.tile([P, PASSES, WIDTH, PACK], BF16, align_bytes=64)
         g_grouped = keep.tile([P, PASSES, WIDTH, PACK], BF16, align_bytes=64)
         z_codes = keep.tile([P, PASSES, WIDTH], U32, align_bytes=64)
@@ -51,26 +53,22 @@ def tile_attention_pa_s_kernel(tc, y_attn, w_proj, b_proj, grad_out, out):
         g_scales = keep.tile([P, PASSES, WIDTH], U8, align_bytes=64)
         acc = [psum.tile([P, WIDTH], F32, name="acc%d" % f) for f in range(F_TILES)]
 
-        for c in range(PASSES):
-            images = slice(c * K_PASS // TOKENS, (c + 1) * K_PASS // TOKENS)
-            nc.sync.dma_start(
-                out=z_raw[:, c].rearrange("p m n i h -> p (m n i h)"),
-                in_=y_attn[images].rearrange("(p m) n x -> p (m n x)", m=IMAGES_PER_PARTITION),
-            )
-        for c in range(PASSES):
-            images = slice(c * K_PASS // TOKENS, (c + 1) * K_PASS // TOKENS)
-            nc.sync.dma_start(
-                out=g_raw[:, c].rearrange("p m i f -> p (m i f)"),
-                in_=grad_out[images].rearrange("(p m) i f -> p (m i f)", m=IMAGES_PER_PARTITION),
-            )
+        images = [slice(c * K_PASS // TOKENS, (c + 1) * K_PASS // TOKENS) for c in range(PASSES)]
+        nc.sync.dma_start(out=z_raw0[:].rearrange("p m n i h -> p (m n i h)"), in_=y_attn[images[0]].rearrange("(p m) n x -> p (m n x)", m=IMAGES_PER_PARTITION))
+        nc.sync.dma_start(out=z_raw1[:].rearrange("p m n i h -> p (m n i h)"), in_=y_attn[images[1]].rearrange("(p m) n x -> p (m n x)", m=IMAGES_PER_PARTITION))
+        nc.sync.dma_start(out=g_raw0[:].rearrange("p m i f -> p (m i f)"), in_=grad_out[images[0]].rearrange("(p m) i f -> p (m i f)", m=IMAGES_PER_PARTITION))
+        nc.sync.dma_start(out=g_raw1[0][:].rearrange("p m i f -> p (m i) f"), in_=grad_out[images[1], :, 0 * HALF : 1 * HALF].rearrange("(p m) i f -> p (m i) f", m=IMAGES_PER_PARTITION))
+        nc.sync.dma_start(out=g_raw1[1][:].rearrange("p m i f -> p (m i) f"), in_=grad_out[images[1], :, 1 * HALF : 2 * HALF].rearrange("(p m) i f -> p (m i) f", m=IMAGES_PER_PARTITION))
 
         def regroup_piece(copy, operand, c, index):
             if operand == "z":
                 cols = slice(index * HALF, (index + 1) * HALF)
-                regroup(copy, z_grouped[:, c, cols, :], z_raw[:, c, :, index])
+                rows = z_raw0[:, :, index] if c == 0 else z_raw1[:, :, index]
+                regroup(copy, z_grouped[:, c, cols, :], rows)
             else:
                 cols = slice(index * P, (index + 1) * P)
-                regroup(copy, g_grouped[:, c, cols, :], g_raw[:, c, :, :, cols])
+                rows = g_raw0[:, :, :, cols] if c == 0 else g_raw1[index // 2][:, :, :, (index % 2) * P : (index % 2 + 1) * P]
+                regroup(copy, g_grouped[:, c, cols, :], rows)
 
         def quantise_piece(operand, c, index):
             if operand == "z":

@@ -42,7 +42,7 @@ def tile_attention_pa_s_kernel(tc, y_attn, w_proj, b_proj, grad_out, out):
         ctx.enter_context(tc.manual_schedule())
 
         z_raw0 = keep.tile([P, IMAGES_PER_PARTITION, TOKENS, TOKENS, HALF], BF16, name="z_raw0")
-        g_raw0 = keep.tile([P, IMAGES_PER_PARTITION, TOKENS, WIDTH], BF16, name="g_raw0")
+        g_raw0 = [keep.tile([P, IMAGES_PER_PARTITION, TOKENS, HALF], BF16, name="g_raw0_%d" % side) for side in range(2)]
         z_raw1 = keep.tile([P, IMAGES_PER_PARTITION, TOKENS, TOKENS, HALF], BF16, name="z_raw1")
         g_raw1 = [keep.tile([P, IMAGES_PER_PARTITION, TOKENS, HALF], BF16, name="g_raw1_%d" % side) for side in range(2)]
         z_grouped = keep.tile([P, PASSES, WIDTH, PACK], BF16, align_bytes=64)
@@ -56,8 +56,9 @@ def tile_attention_pa_s_kernel(tc, y_attn, w_proj, b_proj, grad_out, out):
         images = [slice(c * K_PASS // TOKENS, (c + 1) * K_PASS // TOKENS) for c in range(PASSES)]
         nc.sync.dma_start(out=z_raw0[:].rearrange("p m n i h -> p (m n i h)"), in_=y_attn[images[0]].rearrange("(p m) n x -> p (m n x)", m=IMAGES_PER_PARTITION))
         nc.sync.dma_start(out=z_raw1[:].rearrange("p m n i h -> p (m n i h)"), in_=y_attn[images[1]].rearrange("(p m) n x -> p (m n x)", m=IMAGES_PER_PARTITION))
-        nc.sync.dma_start(out=g_raw0[:].rearrange("p m i f -> p (m i f)"), in_=grad_out[images[0]].rearrange("(p m) i f -> p (m i f)", m=IMAGES_PER_PARTITION))
+        nc.sync.dma_start(out=g_raw0[0][:].rearrange("p m i f -> p (m i) f"), in_=grad_out[images[0], :, 0 * HALF : 1 * HALF].rearrange("(p m) i f -> p (m i) f", m=IMAGES_PER_PARTITION))
         nc.sync.dma_start(out=g_raw1[0][:].rearrange("p m i f -> p (m i) f"), in_=grad_out[images[1], :, 0 * HALF : 1 * HALF].rearrange("(p m) i f -> p (m i) f", m=IMAGES_PER_PARTITION))
+        nc.sync.dma_start(out=g_raw0[1][:].rearrange("p m i f -> p (m i) f"), in_=grad_out[images[0], :, 1 * HALF : 2 * HALF].rearrange("(p m) i f -> p (m i) f", m=IMAGES_PER_PARTITION))
         nc.sync.dma_start(out=g_raw1[1][:].rearrange("p m i f -> p (m i) f"), in_=grad_out[images[1], :, 1 * HALF : 2 * HALF].rearrange("(p m) i f -> p (m i) f", m=IMAGES_PER_PARTITION))
 
         def regroup_piece(copy, operand, c, index):
@@ -67,7 +68,7 @@ def tile_attention_pa_s_kernel(tc, y_attn, w_proj, b_proj, grad_out, out):
                 regroup(copy, z_grouped[:, c, cols, :], rows)
             else:
                 cols = slice(index * P, (index + 1) * P)
-                rows = g_raw0[:, :, :, cols] if c == 0 else g_raw1[index // 2][:, :, :, (index % 2) * P : (index % 2 + 1) * P]
+                rows = g_raw0[index // 2][:, :, :, (index % 2) * P : (index % 2 + 1) * P] if c == 0 else g_raw1[index // 2][:, :, :, (index % 2) * P : (index % 2 + 1) * P]
                 regroup(copy, g_grouped[:, c, cols, :], rows)
 
         def quantise_piece(operand, c, index):

@@ -28,8 +28,8 @@ BYTES = 2 * ROWS * WIDTH * 2 + WIDTH * WIDTH * 4
 
 def regroup(copy, grouped, rows):
     copy(
-        out=grouped.rearrange("p (c r) (m i) -> p c m i r", r=4, i=TOKENS),
-        in_=rows.rearrange("p m i (c r) -> p c m i r", r=4),
+        out=grouped.rearrange("p (c r) (m i) -> p c m i r", r=8, i=TOKENS),
+        in_=rows.rearrange("p m i (c r) -> p c m i r", r=8),
     )
 
 

@@ -44,7 +44,8 @@ def tile_attention_pa_s_kernel(tc, y_attn, w_proj, b_proj, grad_out, out):
         z_raw0 = keep.tile([P, IMAGES_PER_PARTITION, TOKENS, TOKENS, HALF], BF16, name="z_raw0")
         g_raw0 = [keep.tile([P, IMAGES_PER_PARTITION, TOKENS, HALF], BF16, name="g_raw0_%d" % side) for side in range(2)]
         z_raw1 = keep.tile([P, IMAGES_PER_PARTITION, TOKENS, TOKENS, HALF], BF16, name="z_raw1")
-        g_raw1 = [keep.tile([P, IMAGES_PER_PARTITION, TOKENS, HALF], BF16, name="g_raw1_%d" % side) for side in range(2)]
+        g_raw1 = [keep.tile([P, IMAGES_PER_PARTITION, TOKENS, HALF], BF16, name="g_raw1_0")]
+        g_raw1 += [keep.tile([P, IMAGES_PER_PARTITION, TOKENS, P], BF16, name="g_raw1_%d" % f) for f in (2, 3)]
         z_grouped = keep.tile([P, PASSES, WIDTH, PACK], BF16, align_bytes=64)
         g_grouped = keep.tile([P, PASSES, WIDTH, PACK], BF16, align_bytes=64)
         z_codes = keep.tile([P, PASSES, WIDTH], U32, align_bytes=64)
@@ -59,7 +60,8 @@ def tile_attention_pa_s_kernel(tc, y_attn, w_proj, b_proj, grad_out, out):
         nc.sync.dma_start(out=g_raw0[0][:].rearrange("p m i f -> p (m i) f"), in_=grad_out[images[0], :, 0 * HALF : 1 * HALF].rearrange("(p m) i f -> p (m i) f", m=IMAGES_PER_PARTITION))
         nc.sync.dma_start(out=g_raw1[0][:].rearrange("p m i f -> p (m i) f"), in_=grad_out[images[1], :, 0 * HALF : 1 * HALF].rearrange("(p m) i f -> p (m i) f", m=IMAGES_PER_PARTITION))
         nc.sync.dma_start(out=g_raw0[1][:].rearrange("p m i f -> p (m i) f"), in_=grad_out[images[0], :, 1 * HALF : 2 * HALF].rearrange("(p m) i f -> p (m i) f", m=IMAGES_PER_PARTITION))
-        nc.sync.dma_start(out=g_raw1[1][:].rearrange("p m i f -> p (m i) f"), in_=grad_out[images[1], :, 1 * HALF : 2 * HALF].rearrange("(p m) i f -> p (m i) f", m=IMAGES_PER_PARTITION))
+        for f in (2, 3):
+            nc.sync.dma_start(out=g_raw1[f - 1][:].rearrange("p m i f -> p (m i) f"), in_=grad_out[images[1], :, f * P : (f + 1) * P].rearrange("(p m) i f -> p (m i) f", m=IMAGES_PER_PARTITION))
 
         def regroup_piece(copy, operand, c, index):
             if operand == "z":
@@ -68,7 +70,10 @@ def tile_attention_pa_s_kernel(tc, y_attn, w_proj, b_proj, grad_out, out):
                 regroup(copy, z_grouped[:, c, cols, :], rows)
             else:
                 cols = slice(index * P, (index + 1) * P)
-                rows = g_raw0[index // 2][:, :, :, (index % 2) * P : (index % 2 + 1) * P] if c == 0 else g_raw1[index // 2][:, :, :, (index % 2) * P : (index % 2 + 1) * P]
+                if c == 1 and index >= 2:
+                    rows = g_raw1[index - 1][:]
+                else:
+                    rows = (g_raw0 if c == 0 else g_raw1)[index // 2][:, :, :, (index % 2) * P : (index % 2 + 1) * P]
                 regroup(copy, g_grouped[:, c, cols, :], rows)
 
         def quantise_piece(operand, c, index):

@@ -63,11 +63,11 @@ def tile_attention_pa_s_kernel(tc, y_attn, w_proj, b_proj, grad_out, out):
         for f in (2, 3):
             nc.sync.dma_start(out=g_raw1[f - 1][:].rearrange("p m i f -> p (m i) f"), in_=grad_out[images[1], :, f * P : (f + 1) * P].rearrange("(p m) i f -> p (m i) f", m=IMAGES_PER_PARTITION))
 
-        def regroup_piece(copy, operand, c, index):
+        def regroup_piece(copy, operand, c, index, part=None):
             if operand == "z":
-                cols = slice(index * HALF, (index + 1) * HALF)
-                rows = z_raw0[:, :, index] if c == 0 else z_raw1[:, :, index]
-                regroup(copy, z_grouped[:, c, cols, :], rows)
+                start, end = (0, HALF) if part is None else (part * P, (part + 1) * P)
+                rows = (z_raw0 if c == 0 else z_raw1)[:, :, index, :, start:end]
+                regroup(copy, z_grouped[:, c, index * HALF + start : index * HALF + end, :], rows)
             else:
                 cols = slice(index * P, (index + 1) * P)
                 if c == 1 and index >= 2:
@@ -141,7 +141,8 @@ def tile_attention_pa_s_kernel(tc, y_attn, w_proj, b_proj, grad_out, out):
             )
 
         regroup_piece(vector, "z", 0, 0)
-        regroup_piece(scalar, "z", 0, 1)
+        regroup_piece(scalar, "z", 0, 1, 1)
+        regroup_piece(vector, "z", 0, 1, 0)
         quantise_piece("z", 0, 0)
         regroup_piece(vector, "z", 1, 0)
         quantise_piece("z", 0, 1)

@@ -167,5 +167,5 @@ def tile_attention_pa_s_kernel(tc, y_attn, w_proj, b_proj, grad_out, out):
         quantise_piece("g", 0, 3)
         leave(scalar, 1)
         quantise_piece("g", 1, 3)
-        leave(scalar, 2)
-        leave(vector, 3)
+        leave(vector, 2)
+        leave(scalar, 3)

from contextlib import ExitStack

import concourse.mybir as mybir

BF16 = mybir.dt.bfloat16
F32 = mybir.dt.float32
U32 = mybir.dt.uint32
U8 = mybir.dt.uint8
E4M3_X4 = mybir.dt.float8_e4m3fn_x4
E5M2_X4 = mybir.dt.float8_e5m2_x4

P = 128
PACK = 4
K_PASS = P * PACK
IMAGES = 512
TOKENS = 2
WIDTH = 512
ROWS = IMAGES * TOKENS
PASSES = ROWS // K_PASS
IMAGES_PER_PARTITION = PACK // TOKENS
HALF = WIDTH // 2
F_TILES = WIDTH // P
IDLE_PASSES = 13

FLOPS = 2 * ROWS * WIDTH * WIDTH
BYTES = 2 * ROWS * WIDTH * 2 + WIDTH * WIDTH * 4


def regroup(copy, grouped, rows):
    copy(
        out=grouped.rearrange("p (c r) (m i) -> p c m i r", r=8, i=TOKENS),
        in_=rows.rearrange("p m i (c r) -> p c m i r", r=8),
    )


def tile_attention_pa_s_kernel(tc, y_attn, w_proj, b_proj, grad_out, out):
    nc = tc.nc

    with ExitStack() as ctx:
        keep = ctx.enter_context(tc.tile_pool(name="keep", bufs=1))
        psum = ctx.enter_context(tc.psum_pool(name="psum", bufs=1))
        ctx.enter_context(tc.manual_schedule())

        z_raw0 = keep.tile([P, IMAGES_PER_PARTITION, TOKENS, TOKENS, HALF], BF16, name="z_raw0")
        g_raw0 = [keep.tile([P, IMAGES_PER_PARTITION, TOKENS, HALF], BF16, name="g_raw0_%d" % side) for side in range(2)]
        z_raw1 = keep.tile([P, IMAGES_PER_PARTITION, TOKENS, TOKENS, HALF], BF16, name="z_raw1")
        g_raw1 = [keep.tile([P, IMAGES_PER_PARTITION, TOKENS, HALF], BF16, name="g_raw1_0")]
        g_raw1 += [keep.tile([P, IMAGES_PER_PARTITION, TOKENS, P], BF16, name="g_raw1_%d" % f) for f in (2, 3)]
        z_grouped = keep.tile([P, PASSES, WIDTH, PACK], BF16, align_bytes=64)
        g_grouped = keep.tile([P, PASSES, WIDTH, PACK], BF16, align_bytes=64)
        z_codes = keep.tile([P, PASSES, WIDTH], U32, align_bytes=64)
        z_scales = keep.tile([P, PASSES, WIDTH], U8, align_bytes=64)
        g_codes = keep.tile([P, PASSES, WIDTH], U32, align_bytes=64)
        g_scales = keep.tile([P, PASSES, WIDTH], U8, align_bytes=64)
        acc = [psum.tile([P, WIDTH], F32, name="acc%d" % f) for f in range(F_TILES)]

        images = [slice(c * K_PASS // TOKENS, (c + 1) * K_PASS // TOKENS) for c in range(PASSES)]
        nc.sync.dma_start(out=z_raw0[:].rearrange("p m n i h -> p (m n i h)"), in_=y_attn[images[0]].rearrange("(p m) n x -> p (m n x)", m=IMAGES_PER_PARTITION))
        nc.sync.dma_start(out=z_raw1[:].rearrange("p m n i h -> p (m n i h)"), in_=y_attn[images[1]].rearrange("(p m) n x -> p (m n x)", m=IMAGES_PER_PARTITION))
        nc.sync.dma_start(out=g_raw0[0][:].rearrange("p m i f -> p (m i) f"), in_=grad_out[images[0], :, 0 * HALF : 1 * HALF].rearrange("(p m) i f -> p (m i) f", m=IMAGES_PER_PARTITION))
        nc.sync.dma_start(out=g_raw1[0][:].rearrange("p m i f -> p (m i) f"), in_=grad_out[images[1], :, 0 * HALF : 1 * HALF].rearrange("(p m) i f -> p (m i) f", m=IMAGES_PER_PARTITION))
        nc.sync.dma_start(out=g_raw0[1][:].rearrange("p m i f -> p (m i) f"), in_=grad_out[images[0], :, 1 * HALF : 2 * HALF].rearrange("(p m) i f -> p (m i) f", m=IMAGES_PER_PARTITION))
        for f in (2, 3):
            nc.sync.dma_start(out=g_raw1[f - 1][:].rearrange("p m i f -> p (m i) f"), in_=grad_out[images[1], :, f * P : (f + 1) * P].rearrange("(p m) i f -> p (m i) f", m=IMAGES_PER_PARTITION))

        def regroup_piece(copy, operand, c, index, part=None):
            if operand == "z":
                start, end = (0, HALF) if part is None else (part * P, (part + 1) * P)
                rows = (z_raw0 if c == 0 else z_raw1)[:, :, index, :, start:end]
                regroup(copy, z_grouped[:, c, index * HALF + start : index * HALF + end, :], rows)
            else:
                cols = slice(index * P, (index + 1) * P)
                if c == 1 and index >= 2:
                    rows = g_raw1[index - 1][:]
                else:
                    rows = (g_raw0 if c == 0 else g_raw1)[index // 2][:, :, :, (index % 2) * P : (index % 2 + 1) * P]
                regroup(copy, g_grouped[:, c, cols, :], rows)

        def quantise_piece(operand, c, index):
            if operand == "z":
                cols = slice(index * HALF, (index + 1) * HALF)
                nc.vector.quantize_mx(
                    out=z_codes[:, c, cols].bitcast(E4M3_X4),
                    scales=z_scales[:, c, cols],
                    in_=z_grouped[:, c, cols, :].rearrange("p w s -> p (w s)"),
                )
            else:
                cols = slice(index * P, (index + 1) * P)
                nc.vector.quantize_mx(
                    out=g_codes[:, c, cols].bitcast(E5M2_X4),
                    scales=g_scales[:, c, cols],
                    in_=g_grouped[:, c, cols, :].rearrange("p w s -> p (w s)"),
                )
                nc.tensor.matmul_mx(
                    out=acc[index][:],
                    lhsT=g_codes[:, c, cols].bitcast(E5M2_X4),
                    lhsT_scale=g_scales[:, c, cols],
                    rhs=z_codes[:, c, :].bitcast(E4M3_X4),
                    rhs_scale=z_scales[:, c, :],
                    start=(c == 0),
                    stop=(c == PASSES - 1),
                )

        def leave(copy, f):
            result = keep.tile([P, WIDTH], F32, name="result%d" % f)
            by_parity = acc[f][:].rearrange("p (n h) -> p h n", n=TOKENS)
            for part in range(2):
                j_cols = slice(part * HALF, (part + 1) * HALF)
                h_cols = slice(part * HALF // TOKENS, (part + 1) * HALF // TOKENS)
                copy(
                    out=result[:, j_cols].rearrange("p (h n) -> p h n", n=TOKENS),
                    in_=by_parity[:, h_cols, :],
                )
                nc.sync.dma_start(out=out[f * P : (f + 1) * P, j_cols], in_=result[:, j_cols])

        vector = nc.vector.tensor_copy
        scalar = nc.scalar.copy

        zeros = keep.tile([P, P * PACK], BF16, align_bytes=64)
        idle_z_codes = keep.tile([P, WIDTH], U32, align_bytes=64)
        idle_z_scales = keep.tile([P, WIDTH], U8, align_bytes=64)
        idle_g_codes = keep.tile([P, P], U32, align_bytes=64)
        idle_g_scales = keep.tile([P, P], U8, align_bytes=64)
        idle = psum.tile([P, WIDTH], F32, name="idle")
        nc.vector.memset(zeros[:], 0.0)
        nc.vector.quantize_mx(out=idle_g_codes[:].bitcast(E5M2_X4), scales=idle_g_scales[:], in_=zeros[:])
        for f in range(F_TILES):
            cols = slice(f * P, (f + 1) * P)
            nc.vector.quantize_mx(
                out=idle_z_codes[:, cols].bitcast(E4M3_X4), scales=idle_z_scales[:, cols], in_=zeros[:]
            )
        for repeat in range(IDLE_PASSES):
            nc.tensor.matmul_mx(
                out=idle[:],
                lhsT=idle_g_codes[:].bitcast(E5M2_X4),
                lhsT_scale=idle_g_scales[:],
                rhs=idle_z_codes[:].bitcast(E4M3_X4),
                rhs_scale=idle_z_scales[:],
                start=True,
                stop=True,
            )

        regroup_piece(vector, "z", 0, 0)
        regroup_piece(scalar, "z", 0, 1, 1)
        regroup_piece(vector, "z", 0, 1, 0)
        quantise_piece("z", 0, 0)
        regroup_piece(vector, "z", 1, 0)
        quantise_piece("z", 0, 1)
        regroup_piece(scalar, "z", 1, 1)
        quantise_piece("z", 1, 0)
        regroup_piece(vector, "g", 0, 0)
        quantise_piece("z", 1, 1)
        regroup_piece(scalar, "g", 0, 1)
        regroup_piece(vector, "g", 1, 0)
        quantise_piece("g", 0, 0)
        quantise_piece("g", 1, 0)
        regroup_piece(scalar, "g", 1, 1)
        quantise_piece("g", 0, 1)
        regroup_piece(vector, "g", 0, 2)
        quantise_piece("g", 1, 1)
        regroup_piece(scalar, "g", 0, 3)
        regroup_piece(vector, "g", 1, 2)
        quantise_piece("g", 0, 2)
        quantise_piece("g", 1, 2)
        leave(scalar, 0)
        regroup_piece(vector, "g", 1, 3)
        quantise_piece("g", 0, 3)
        leave(scalar, 1)
        quantise_piece("g", 1, 3)
        leave(vector, 2)
        leave(scalar, 3)
